import numpy as np
import ml_dtypes


def mxq(x, axis, fmt="e4m3"):
    dtype, down = {"e4m3": (ml_dtypes.float8_e4m3fn, 7), "e5m2": (ml_dtypes.float8_e5m2, 14)}[fmt]
    v = np.moveaxis(np.asarray(x, np.float32).astype(ml_dtypes.bfloat16).astype(np.float64), axis, -1)
    blocks = v.reshape(v.shape[:-1] + (-1, 32))
    amax = np.abs(blocks).max(-1, keepdims=True)
    byte = np.maximum(np.where(amax > 0, np.frexp(amax)[1] - 1 + 127, 0) - down, 1)
    scale = np.exp2(byte - 127.0)
    codes = (blocks / scale).astype(np.float32).astype(dtype).astype(np.float64)
    return np.moveaxis((codes * scale).reshape(v.shape), -1, axis)


WIDE = False


def mx_kscale(k):
    if not WIDE:
        return np.ones(k)
    levels = np.array([10, -10, 5, -5, 0])
    a = np.random.permutation(np.resize(levels, k // 512 * 4)).reshape(k // 512, 4)
    idx = np.arange(k)
    return np.exp2(a[idx // 512, idx % 128 // 32])


BF16 = ml_dtypes.bfloat16


def bf(x):
    return np.asarray(x, np.float32).astype(BF16)


def f64(x):
    return np.asarray(x).astype(np.float64)


B, T, C, HS, DW, DA, DV, DG = 4, 128, 2048, 64, 512, 128, 128, 224
H = C // HS


def setup_inputs():
    s = mx_kscale(C)
    return {
        "x": bf(np.random.standard_normal((B, T, C)) * s),
        "x_k": bf(np.random.uniform(0.0, 1.0, C)),
        "Wk": bf(np.random.standard_normal((C, C)) / np.sqrt(C) / s[None, :]),
        "k_k": bf(0.71 + 0.1 * np.random.standard_normal(C)),
    }


def reference(x, x_k, Wk, k_k):
    x = f64(x)
    xprev = np.concatenate([np.zeros_like(x[:, :1]), x[:, :-1]], axis=1)
    xx = xprev - x
    xk = x + xx * f64(x_k)
    k = mxq(xk, 2, "e4m3") @ mxq(f64(Wk), 1, "e4m3").T
    kk4 = (k * f64(k_k)).reshape(B, T, H, HS)
    nrm = np.sqrt((kk4 ** 2).sum(-1, keepdims=True))
    kk = (kk4 / np.maximum(nrm, 1e-12)).reshape(B, T, C)
    return kk

@@ -1,0 +1,182 @@
+from contextlib import ExitStack
+
+import concourse.mybir as mybir
+from concourse.masks import make_identity
+
+F32 = mybir.dt.float32
+BF16 = mybir.dt.bfloat16
+U32 = mybir.dt.uint32
+U8 = mybir.dt.uint8
+FP8X4 = mybir.dt.float8_e4m3fn_x4
+ACT = mybir.ActivationFunctionType
+ALU = mybir.AluOpType
+
+P = 128
+B = 4
+T = 128
+C = 2048
+HEAD = 64
+PACK = 4
+PAIR = 2
+HALVES = PACK // PAIR
+K_PASS = P * PACK
+PASSES = C // K_PASS
+N_CHUNK = 512
+CHUNKS = C // N_CHUNK
+ROW_TILES = N_CHUNK // P
+HEADS = N_CHUNK // HEAD
+BANK_PASSES = 2
+
+FLOPS = 2 * B * T * C * C
+
+
+def tile_full_tmix_params_pa_kernel(tc, x, x_k, Wk, k_k, out):
+    nc = tc.nc
+    with ExitStack() as ctx:
+        const = ctx.enter_context(tc.tile_pool(name="const", bufs=1))
+        inputs = ctx.enter_context(tc.tile_pool(name="inputs", bufs=1))
+        x_work = ctx.enter_context(tc.tile_pool(name="x_work", bufs=2))
+        w_work = ctx.enter_context(tc.tile_pool(name="w_work", bufs=2))
+        epilogue = ctx.enter_context(tc.tile_pool(name="epilogue", bufs=4))
+        turned = ctx.enter_context(tc.psum_pool(name="turned", bufs=4))
+        sums = ctx.enter_context(tc.psum_pool(name="sums", bufs=4))
+
+        mix_bf = const.tile([P, PASSES * HALVES, PAIR], BF16)
+        with nc.allow_non_contiguous_dma(reason="x_k: 4 KiB, one word of two channels a piece"):
+            nc.scalar.dma_start(out=mix_bf[:], in_=x_k.rearrange("(a p e) -> p a e", p=P, e=PAIR))
+        x_sb = [inputs.tile([P, C], BF16, name="x_sb%d" % b) for b in range(B)]
+        for b in range(B):
+            nc.sync.dma_start(out=x_sb[b][:], in_=x[b])
+        w_sb = [inputs.tile([P, C], BF16, name="w_sb%d" % r) for r in range(C // P)]
+        gain = const.tile([P, C], BF16)
+        for r in range(C // P):
+            nc.sync.dma_start(out=w_sb[r][:], in_=Wk[r * P : (r + 1) * P, :])
+            if r == ROW_TILES - 1:
+                nc.sync.dma_start(out=gain[:], in_=k_k.partition_broadcast(P))
+
+        ident = const.tile([P, P], F32)
+        make_identity(nc, ident[:])
+        warm = const.tile([P, 1], F32)
+        nc.vector.memset(warm[:], 1.0)
+        nc.scalar.sqrt(out=warm[:], in_=warm[:])
+        mix = const.tile([P, PASSES * PACK], F32)
+        keep = const.tile([P, PASSES * PACK], F32)
+        nc.vector.tensor_copy(out=mix[:], in_=mix_bf[:].rearrange("p a e -> p (a e)"))
+        nc.vector.tensor_scalar(
+            out=keep[:], in0=mix[:], scalar1=-1.0, scalar2=1.0, op0=ALU.mult, op1=ALU.add
+        )
+        prev_term = [const.tile([P, PAIR, B, T + 1], F32, name="prev_term%d" % i) for i in range(2)]
+        for i in range(2):
+            nc.vector.memset(prev_term[i][:], 0.0)
+
+        x_codes = const.tile([P, PASSES, B * T], U32, align_bytes=64)
+        x_scales = const.tile([P, PASSES, B * T], U8, align_bytes=64)
+        for g in range(PASSES):
+            planes = x_work.tile([P, PACK, B * T], BF16)
+            for u in range(HALVES):
+                a = HALVES * g + u
+                x_turned = turned.tile([P, B, T], F32, tag="turned")
+                for b in range(B):
+                    nc.tensor.transpose(
+                        x_turned[:, b, :], x_sb[b][:].bitcast(F32)[:, a * P : (a + 1) * P], ident[:]
+                    )
+                x_halves = x_turned[:].bitcast(BF16).rearrange("p b (s e) -> p b s e", e=PAIR)
+                shifted = prev_term[a % 2]
+                for e in range(PAIR):
+                    col = PAIR * a + e
+                    nc.scalar.activation(
+                        out=shifted[:, e, :, 1 : T + 1],
+                        in_=x_halves[:, :, :, e],
+                        func=ACT.Copy,
+                        scale=mix[:, col : col + 1],
+                    )
+                for e in range(PAIR):
+                    col = PAIR * a + e
+                    nc.vector.scalar_tensor_tensor(
+                        out=planes[:, PAIR * u + e, :].rearrange("p (b s) -> p b s", b=B),
+                        in0=x_halves[:, :, :, e],
+                        scalar=keep[:, col : col + 1],
+                        in1=shifted[:, e, :, 0:T],
+                        op0=ALU.mult,
+                        op1=ALU.add,
+                    )
+            x_grouped = x_work.tile([P, B * T, PACK], BF16, align_bytes=64)
+            nc.vector.tensor_copy(out=x_grouped[:], in_=planes[:].rearrange("p t c -> p c t"))
+            nc.vector.quantize_mx(
+                out=x_codes[:, g, :].bitcast(FP8X4),
+                scales=x_scales[:, g, :],
+                in_=x_grouped[:].rearrange("p c t -> p (c t)"),
+            )
+
+        def quantise_w_chunk(n):
+            w_grouped = w_work.tile([P, PASSES, N_CHUNK, PACK], BF16, align_bytes=64)
+            w_words = w_grouped[:].bitcast(F32)
+            w_codes = w_work.tile([P, PASSES, N_CHUNK], U32, align_bytes=64)
+            w_scales = w_work.tile([P, PASSES, N_CHUNK], U8, align_bytes=64)
+            for j in range(ROW_TILES):
+                rows = w_sb[ROW_TILES * n + j][:].bitcast(F32)
+                for first in range(0, PASSES, BANK_PASSES):
+                    w_turned = turned.tile([P, BANK_PASSES, HALVES, P], F32, tag="turned")
+                    for i in range(BANK_PASSES):
+                        for u in range(HALVES):
+                            a = HALVES * (first + i) + u
+                            nc.tensor.transpose(
+                                w_turned[:, i, u, :], rows[:, a * P : (a + 1) * P], ident[:]
+                            )
+                    nc.scalar.copy(
+                        out=w_words[:, first : first + BANK_PASSES, j * P : (j + 1) * P, :],
+                        in_=w_turned[:].rearrange("p i u o -> p i o u"),
+                    )
+            for g in range(PASSES):
+                nc.vector.quantize_mx(
+                    out=w_codes[:, g, :].bitcast(FP8X4),
+                    scales=w_scales[:, g, :],
+                    in_=w_grouped[:, g, :, :].rearrange("p c t -> p (c t)"),
+                )
+            return w_codes, w_scales
+
+        def multiply_and_normalise(n, w_codes, w_scales):
+            cols = slice(n * N_CHUNK, (n + 1) * N_CHUNK)
+            for b in range(B):
+                toks = slice(b * T, (b + 1) * T)
+                acc = sums.tile([P, N_CHUNK], F32)
+                for g in range(PASSES):
+                    nc.tensor.matmul_mx(
+                        out=acc[:],
+                        lhsT=x_codes[:, g, toks].bitcast(FP8X4),
+                        lhsT_scale=x_scales[:, g, toks],
+                        rhs=w_codes[:, g, :].bitcast(FP8X4),
+                        rhs_scale=w_scales[:, g, :],
+                        start=(g == 0),
+                        stop=(g == PASSES - 1),
+                    )
+                kk = epilogue.tile([P, HEADS, HEAD], F32)
+                nc.vector.tensor_tensor(
+                    out=kk[:].rearrange("p h d -> p (h d)"), in0=acc[:], in1=gain[:, cols], op=ALU.mult
+                )
+                squares = epilogue.tile([P, HEADS, HEAD], F32)
+                sumsq = epilogue.tile([P, HEADS], F32)
+                for h in range(HEADS):
+                    nc.scalar.activation(
+                        out=squares[:, h, :], in_=kk[:, h, :], func=ACT.Square,
+                        accum_out=sumsq[:, h : h + 1],
+                    )
+                floored = epilogue.tile([P, HEADS], F32)
+                nc.vector.tensor_scalar_max(out=floored[:], in0=sumsq[:], scalar1=1e-24)
+                norm = epilogue.tile([P, HEADS], F32)
+                nc.scalar.sqrt(out=norm[:], in_=floored[:])
+                inverse = epilogue.tile([P, HEADS], F32)
+                nc.vector.reciprocal(out=inverse[:], in_=norm[:])
+                nc.vector.tensor_tensor(
+                    out=kk[:],
+                    in0=kk[:],
+                    in1=inverse[:].unsqueeze(2).to_broadcast([P, HEADS, HEAD]),
+                    op=ALU.mult,
+                )
+                nc.sync.dma_start(out=out[b, :, cols], in_=kk[:].rearrange("p h d -> p (h d)"))
+
+        ready = quantise_w_chunk(0)
+        for n in range(CHUNKS):
+            following = quantise_w_chunk(n + 1) if n + 1 < CHUNKS else None
+            multiply_and_normalise(n, ready[0], ready[1])
+            ready = following

@@ -25,7 +25,8 @@ N_CHUNK = 512
 CHUNKS = C // N_CHUNK
 ROW_TILES = N_CHUNK // P
 HEADS = N_CHUNK // HEAD
-BANK_PASSES = 2
+BANK_TILES = 2
+STEP = 2
 
 FLOPS = 2 * B * T * C * C
 
@@ -33,20 +34,25 @@ FLOPS = 2 * B * T * C * C
 def tile_full_tmix_params_pa_kernel(tc, x, x_k, Wk, k_k, out):
     nc = tc.nc
     with ExitStack() as ctx:
+        ctx.enter_context(tc.manual_schedule())
         const = ctx.enter_context(tc.tile_pool(name="const", bufs=1))
         inputs = ctx.enter_context(tc.tile_pool(name="inputs", bufs=1))
         x_work = ctx.enter_context(tc.tile_pool(name="x_work", bufs=2))
         w_work = ctx.enter_context(tc.tile_pool(name="w_work", bufs=2))
-        epilogue = ctx.enter_context(tc.tile_pool(name="epilogue", bufs=4))
+        results = ctx.enter_context(tc.tile_pool(name="results", bufs=8))
+        scratch = ctx.enter_context(tc.tile_pool(name="scratch", bufs=4))
         turned = ctx.enter_context(tc.psum_pool(name="turned", bufs=4))
         sums = ctx.enter_context(tc.psum_pool(name="sums", bufs=4))
 
         mix_bf = const.tile([P, PASSES * HALVES, PAIR], BF16)
         with nc.allow_non_contiguous_dma(reason="x_k: 4 KiB, one word of two channels a piece"):
             nc.scalar.dma_start(out=mix_bf[:], in_=x_k.rearrange("(a p e) -> p a e", p=P, e=PAIR))
-        x_sb = [inputs.tile([P, C], BF16, name="x_sb%d" % b) for b in range(B)]
-        for b in range(B):
-            nc.sync.dma_start(out=x_sb[b][:], in_=x[b])
+        x_sb = [inputs.tile([P, B, K_PASS], BF16, name="x_sb%d" % g) for g in range(PASSES)]
+        for g in range(PASSES):
+            nc.sync.dma_start(
+                out=x_sb[g][:],
+                in_=x[:, :, g * K_PASS : (g + 1) * K_PASS].rearrange("b s k -> s b k"),
+            )
         w_sb = [inputs.tile([P, C], BF16, name="w_sb%d" % r) for r in range(C // P)]
         gain = const.tile([P, C], BF16)
         for r in range(C // P):
@@ -58,30 +64,38 @@ def tile_full_tmix_params_pa_kernel(tc, x, x_k, Wk, k_k, out):
         make_identity(nc, ident[:])
         warm = const.tile([P, 1], F32)
         nc.vector.memset(warm[:], 1.0)
-        nc.scalar.sqrt(out=warm[:], in_=warm[:])
+        nc.scalar.activation(out=warm[:], in_=warm[:], func=ACT.Abs_reciprocal_sqrt)
+        prev_term = [
+            const.tile([P, PAIR, B, T + 1], F32, name="prev_term%d" % i) for i in range(PASSES)
+        ]
+        for i in range(PASSES):
+            nc.vector.memset(prev_term[i][:], 0.0)
         mix = const.tile([P, PASSES * PACK], F32)
         keep = const.tile([P, PASSES * PACK], F32)
         nc.vector.tensor_copy(out=mix[:], in_=mix_bf[:].rearrange("p a e -> p (a e)"))
         nc.vector.tensor_scalar(
             out=keep[:], in0=mix[:], scalar1=-1.0, scalar2=1.0, op0=ALU.mult, op1=ALU.add
         )
-        prev_term = [const.tile([P, PAIR, B, T + 1], F32, name="prev_term%d" % i) for i in range(2)]
-        for i in range(2):
-            nc.vector.memset(prev_term[i][:], 0.0)
 
         x_codes = const.tile([P, PASSES, B * T], U32, align_bytes=64)
         x_scales = const.tile([P, PASSES, B * T], U8, align_bytes=64)
-        for g in range(PASSES):
+
+        x_turned = []
+        for a in range(PASSES * HALVES):
+            pool = turned if a % HALVES == 0 else sums
+            bank = pool.tile([P, B, T], F32, name="x_turned", tag="bank")
+            for b in range(B):
+                words = x_sb[a // HALVES][:, b, :].bitcast(F32)
+                u = a % HALVES
+                nc.tensor.transpose(bank[:, b, :], words[:, u * P : (u + 1) * P], ident[:])
+            x_turned.append(bank)
+
+        def mix_x(g):
             planes = x_work.tile([P, PACK, B * T], BF16)
             for u in range(HALVES):
                 a = HALVES * g + u
-                x_turned = turned.tile([P, B, T], F32, tag="turned")
-                for b in range(B):
-                    nc.tensor.transpose(
-                        x_turned[:, b, :], x_sb[b][:].bitcast(F32)[:, a * P : (a + 1) * P], ident[:]
-                    )
-                x_halves = x_turned[:].bitcast(BF16).rearrange("p b (s e) -> p b s e", e=PAIR)
-                shifted = prev_term[a % 2]
+                x_halves = x_turned[a][:].bitcast(BF16).rearrange("p b (s e) -> p b s e", e=PAIR)
+                shifted = prev_term[a % PASSES]
                 for e in range(PAIR):
                     col = PAIR * a + e
                     nc.scalar.activation(
@@ -101,82 +115,126 @@ def tile_full_tmix_params_pa_kernel(tc, x, x_k, Wk, k_k, out):
                         op1=ALU.add,
                     )
             x_grouped = x_work.tile([P, B * T, PACK], BF16, align_bytes=64)
-            nc.vector.tensor_copy(out=x_grouped[:], in_=planes[:].rearrange("p t c -> p c t"))
+            nc.vector.tensor_copy(
+                out=x_grouped[:].rearrange("p (c i) t -> p c t i", i=4),
+                in_=planes[:].rearrange("p t (c i) -> p c t i", i=4),
+            )
+            return x_grouped
+
+        def quantise_x(g, x_grouped):
             nc.vector.quantize_mx(
                 out=x_codes[:, g, :].bitcast(FP8X4),
                 scales=x_scales[:, g, :],
                 in_=x_grouped[:].rearrange("p c t -> p (c t)"),
             )
 
-        def quantise_w_chunk(n):
-            w_grouped = w_work.tile([P, PASSES, N_CHUNK, PACK], BF16, align_bytes=64)
-            w_words = w_grouped[:].bitcast(F32)
-            w_codes = w_work.tile([P, PASSES, N_CHUNK], U32, align_bytes=64)
-            w_scales = w_work.tile([P, PASSES, N_CHUNK], U8, align_bytes=64)
-            for j in range(ROW_TILES):
-                rows = w_sb[ROW_TILES * n + j][:].bitcast(F32)
-                for first in range(0, PASSES, BANK_PASSES):
-                    w_turned = turned.tile([P, BANK_PASSES, HALVES, P], F32, tag="turned")
-                    for i in range(BANK_PASSES):
-                        for u in range(HALVES):
-                            a = HALVES * (first + i) + u
-                            nc.tensor.transpose(
-                                w_turned[:, i, u, :], rows[:, a * P : (a + 1) * P], ident[:]
-                            )
-                    nc.scalar.copy(
-                        out=w_words[:, first : first + BANK_PASSES, j * P : (j + 1) * P, :],
-                        in_=w_turned[:].rearrange("p i u o -> p i o u"),
-                    )
+        def new_w_chunk():
+            return {
+                "grouped": w_work.tile([P, PASSES, N_CHUNK, PACK], BF16, name="w_grouped", align_bytes=64),
+                "codes": w_work.tile([P, PASSES, N_CHUNK], U32, name="w_codes", align_bytes=64),
+                "scales": w_work.tile([P, PASSES, N_CHUNK], U8, name="w_scales", align_bytes=64),
+            }
+
+        def turn_w(n, g, chunk, last_copy):
+            w_words = chunk["grouped"][:].bitcast(F32)
+            for first in range(0, ROW_TILES, BANK_TILES):
+                bank = turned.tile([P, HALVES, BANK_TILES, P], F32, name="w_turned", tag="bank")
+                for j in range(BANK_TILES):
+                    rows = w_sb[ROW_TILES * n + first + j][:].bitcast(F32)
+                    for u in range(HALVES):
+                        a = HALVES * g + u
+                        nc.tensor.transpose(bank[:, u, j, :], rows[:, a * P : (a + 1) * P], ident[:])
+                copy = last_copy if first + BANK_TILES == ROW_TILES else nc.scalar.copy
+                copy(
+                    out=w_words[:, g, first * P : (first + BANK_TILES) * P, :],
+                    in_=bank[:].rearrange("p u j o -> p (j o) u"),
+                )
+
+        def quantise_w(g, chunk):
+            nc.vector.quantize_mx(
+                out=chunk["codes"][:, g, :].bitcast(FP8X4),
+                scales=chunk["scales"][:, g, :],
+                in_=chunk["grouped"][:, g, :, :].rearrange("p c t -> p (c t)"),
+            )
+
+        def multiply(b, chunk):
+            toks = slice(b * T, (b + 1) * T)
+            acc = sums.tile([P, N_CHUNK], F32, name="acc", tag="bank")
             for g in range(PASSES):
-                nc.vector.quantize_mx(
-                    out=w_codes[:, g, :].bitcast(FP8X4),
-                    scales=w_scales[:, g, :],
-                    in_=w_grouped[:, g, :, :].rearrange("p c t -> p (c t)"),
+                nc.tensor.matmul_mx(
+                    out=acc[:],
+                    lhsT=x_codes[:, g, toks].bitcast(FP8X4),
+                    lhsT_scale=x_scales[:, g, toks],
+                    rhs=chunk["codes"][:, g, :].bitcast(FP8X4),
+                    rhs_scale=chunk["scales"][:, g, :],
+                    start=(g == 0),
+                    stop=(g == PASSES - 1),
                 )
-            return w_codes, w_scales
+            return acc
 
-        def multiply_and_normalise(n, w_codes, w_scales):
-            cols = slice(n * N_CHUNK, (n + 1) * N_CHUNK)
-            for b in range(B):
-                toks = slice(b * T, (b + 1) * T)
-                acc = sums.tile([P, N_CHUNK], F32)
-                for g in range(PASSES):
-                    nc.tensor.matmul_mx(
-                        out=acc[:],
-                        lhsT=x_codes[:, g, toks].bitcast(FP8X4),
-                        lhsT_scale=x_scales[:, g, toks],
-                        rhs=w_codes[:, g, :].bitcast(FP8X4),
-                        rhs_scale=w_scales[:, g, :],
-                        start=(g == 0),
-                        stop=(g == PASSES - 1),
-                    )
-                kk = epilogue.tile([P, HEADS, HEAD], F32)
-                nc.vector.tensor_tensor(
-                    out=kk[:].rearrange("p h d -> p (h d)"), in0=acc[:], in1=gain[:, cols], op=ALU.mult
-                )
-                squares = epilogue.tile([P, HEADS, HEAD], F32)
-                sumsq = epilogue.tile([P, HEADS], F32)
-                for h in range(HEADS):
-                    nc.scalar.activation(
-                        out=squares[:, h, :], in_=kk[:, h, :], func=ACT.Square,
-                        accum_out=sumsq[:, h : h + 1],
-                    )
-                floored = epilogue.tile([P, HEADS], F32)
-                nc.vector.tensor_scalar_max(out=floored[:], in0=sumsq[:], scalar1=1e-24)
-                norm = epilogue.tile([P, HEADS], F32)
-                nc.scalar.sqrt(out=norm[:], in_=floored[:])
-                inverse = epilogue.tile([P, HEADS], F32)
-                nc.vector.reciprocal(out=inverse[:], in_=norm[:])
-                nc.vector.tensor_tensor(
-                    out=kk[:],
-                    in0=kk[:],
-                    in1=inverse[:].unsqueeze(2).to_broadcast([P, HEADS, HEAD]),
-                    op=ALU.mult,
-                )
-                nc.sync.dma_start(out=out[b, :, cols], in_=kk[:].rearrange("p h d -> p (h d)"))
+        def times_gain(n, acc):
+            kk = results.tile([P, HEADS, HEAD], F32)
+            nc.vector.tensor_tensor(
+                out=kk[:].rearrange("p h d -> p (h d)"),
+                in0=acc[:],
+                in1=gain[:, n * N_CHUNK : (n + 1) * N_CHUNK],
+                op=ALU.mult,
+            )
+            return kk
 
-        ready = quantise_w_chunk(0)
+        def normalise_and_store(n, b, kk):
+            squares = scratch.tile([P, HEADS, HEAD], F32)
+            sumsq = scratch.tile([P, HEADS], F32)
+            for h in range(HEADS):
+                nc.scalar.activation(
+                    out=squares[:, h, :], in_=kk[:, h, :], func=ACT.Square,
+                    accum_out=sumsq[:, h : h + 1],
+                )
+            inverse = scratch.tile([P, HEADS], F32)
+            nc.scalar.activation(out=inverse[:], in_=sumsq[:], func=ACT.Abs_reciprocal_sqrt)
+            capped = scratch.tile([P, HEADS], F32)
+            nc.vector.tensor_scalar_min(out=capped[:], in0=inverse[:], scalar1=1e12)
+            engine = nc.gpsimd if n + 1 < CHUNKS else nc.vector
+            engine.tensor_tensor(
+                out=kk[:],
+                in0=kk[:],
+                in1=capped[:].unsqueeze(2).to_broadcast([P, HEADS, HEAD]),
+                op=ALU.mult,
+            )
+            nc.sync.dma_start(
+                out=out[b, :, n * N_CHUNK : (n + 1) * N_CHUNK], in_=kk[:].rearrange("p h d -> p (h d)")
+            )
+
+        grouped_before = None
+        for g in range(PASSES):
+            x_grouped = mix_x(g)
+            if g > 0:
+                quantise_x(g - 1, grouped_before)
+            grouped_before = x_grouped
+        chunk = new_w_chunk()
+        for g in range(PASSES):
+            turn_w(0, g, chunk, nc.scalar.copy)
+        quantise_x(PASSES - 1, grouped_before)
+        for g in range(PASSES):
+            quantise_w(g, chunk)
+
+        waiting = []
         for n in range(CHUNKS):
-            following = quantise_w_chunk(n + 1) if n + 1 < CHUNKS else None
-            multiply_and_normalise(n, ready[0], ready[1])
-            ready = following
+            following = new_w_chunk() if n + 1 < CHUNKS else None
+            for first in range(0, B, STEP):
+                step = range(first, first + STEP)
+                if following is not None:
+                    for g in step:
+                        last_copy = nc.vector.tensor_copy if g == step[-1] else nc.scalar.copy
+                        turn_w(n + 1, g, following, last_copy)
+                accs = [multiply(b, chunk) for b in step]
+                if following is not None:
+                    for g in step:
+                        quantise_w(g, following)
+                scaled = [(n, b, times_gain(n, acc)) for b, acc in zip(step, accs)]
+                for tile_n, tile_b, kk in waiting:
+                    normalise_and_store(tile_n, tile_b, kk)
+                waiting = scaled
+            chunk = following
+        for tile_n, tile_b, kk in waiting:
+            normalise_and_store(tile_n, tile_b, kk)

@@ -27,6 +27,8 @@ ROW_TILES = N_CHUNK // P
 HEADS = N_CHUNK // HEAD
 BANK_TILES = 2
 STEP = 2
+HEAD_CHUNKS = 2
+GPSIMD_PASSES = 2
 
 FLOPS = 2 * B * T * C * C
 
@@ -37,10 +39,10 @@ def tile_full_tmix_params_pa_kernel(tc, x, x_k, Wk, k_k, out):
         ctx.enter_context(tc.manual_schedule())
         const = ctx.enter_context(tc.tile_pool(name="const", bufs=1))
         inputs = ctx.enter_context(tc.tile_pool(name="inputs", bufs=1))
-        x_work = ctx.enter_context(tc.tile_pool(name="x_work", bufs=2))
+        x_work = ctx.enter_context(tc.tile_pool(name="x_work", bufs=PASSES))
         w_work = ctx.enter_context(tc.tile_pool(name="w_work", bufs=2))
         results = ctx.enter_context(tc.tile_pool(name="results", bufs=8))
-        scratch = ctx.enter_context(tc.tile_pool(name="scratch", bufs=4))
+        scratch = ctx.enter_context(tc.tile_pool(name="scratch", bufs=2))
         turned = ctx.enter_context(tc.psum_pool(name="turned", bufs=4))
         sums = ctx.enter_context(tc.psum_pool(name="sums", bufs=4))
 
@@ -57,7 +59,7 @@ def tile_full_tmix_params_pa_kernel(tc, x, x_k, Wk, k_k, out):
         gain = const.tile([P, C], BF16)
         for r in range(C // P):
             nc.sync.dma_start(out=w_sb[r][:], in_=Wk[r * P : (r + 1) * P, :])
-            if r == ROW_TILES - 1:
+            if r == HEAD_CHUNKS * ROW_TILES - 1:
                 nc.sync.dma_start(out=gain[:], in_=k_k.partition_broadcast(P))
 
         ident = const.tile([P, P], F32)
@@ -114,11 +116,24 @@ def tile_full_tmix_params_pa_kernel(tc, x, x_k, Wk, k_k, out):
                         op0=ALU.mult,
                         op1=ALU.add,
                     )
+            return planes
+
+        def regroup_x(g, planes):
             x_grouped = x_work.tile([P, B * T, PACK], BF16, align_bytes=64)
-            nc.vector.tensor_copy(
-                out=x_grouped[:].rearrange("p (c i) t -> p c t i", i=4),
-                in_=planes[:].rearrange("p t (c i) -> p c t i", i=4),
-            )
+            if g < GPSIMD_PASSES:
+                nc.gpsimd.tensor_scalar(
+                    out=x_grouped[:],
+                    in0=planes[:].rearrange("p t c -> p c t"),
+                    scalar1=1.0,
+                    scalar2=0.0,
+                    op0=ALU.mult,
+                    op1=ALU.add,
+                )
+            else:
+                nc.vector.tensor_copy(
+                    out=x_grouped[:].rearrange("p (c i) t -> p c t i", i=4),
+                    in_=planes[:].rearrange("p t (c i) -> p c t i", i=4),
+                )
             return x_grouped
 
         def quantise_x(g, x_grouped):
@@ -182,59 +197,68 @@ def tile_full_tmix_params_pa_kernel(tc, x, x_k, Wk, k_k, out):
             )
             return kk
 
-        def normalise_and_store(n, b, kk):
-            squares = scratch.tile([P, HEADS, HEAD], F32)
-            sumsq = scratch.tile([P, HEADS], F32)
-            for h in range(HEADS):
-                nc.scalar.activation(
-                    out=squares[:, h, :], in_=kk[:, h, :], func=ACT.Square,
-                    accum_out=sumsq[:, h : h + 1],
-                )
-            inverse = scratch.tile([P, HEADS], F32)
+        def normalise_and_store(n, tiles):
+            squares = scratch.tile([P, STEP, HEADS, HEAD], F32)
+            sumsq = scratch.tile([P, STEP, HEADS], F32)
+            for i, (b, kk) in enumerate(tiles):
+                for h in range(HEADS):
+                    nc.scalar.activation(
+                        out=squares[:, i, h, :], in_=kk[:, h, :], func=ACT.Square,
+                        accum_out=sumsq[:, i, h : h + 1],
+                    )
+            inverse = scratch.tile([P, STEP, HEADS], F32)
             nc.scalar.activation(out=inverse[:], in_=sumsq[:], func=ACT.Abs_reciprocal_sqrt)
-            capped = scratch.tile([P, HEADS], F32)
+            capped = scratch.tile([P, STEP, HEADS], F32)
             nc.vector.tensor_scalar_min(out=capped[:], in0=inverse[:], scalar1=1e12)
             engine = nc.gpsimd if n + 1 < CHUNKS else nc.vector
-            engine.tensor_tensor(
-                out=kk[:],
-                in0=kk[:],
-                in1=capped[:].unsqueeze(2).to_broadcast([P, HEADS, HEAD]),
-                op=ALU.mult,
-            )
-            nc.sync.dma_start(
-                out=out[b, :, n * N_CHUNK : (n + 1) * N_CHUNK], in_=kk[:].rearrange("p h d -> p (h d)")
-            )
+            for i, (b, kk) in enumerate(tiles):
+                engine.tensor_tensor(
+                    out=kk[:],
+                    in0=kk[:],
+                    in1=capped[:, i, :].unsqueeze(2).to_broadcast([P, HEADS, HEAD]),
+                    op=ALU.mult,
+                )
+                nc.sync.dma_start(
+                    out=out[b, :, n * N_CHUNK : (n + 1) * N_CHUNK],
+                    in_=kk[:].rearrange("p h d -> p (h d)"),
+                )
 
-        grouped_before = None
+        chunks = [new_w_chunk() for n in range(HEAD_CHUNKS)]
+        mixed = []
+        regrouped = []
         for g in range(PASSES):
-            x_grouped = mix_x(g)
-            if g > 0:
-                quantise_x(g - 1, grouped_before)
-            grouped_before = x_grouped
-        chunk = new_w_chunk()
+            mixed.append(mix_x(g))
+            if g < GPSIMD_PASSES:
+                regrouped.append(regroup_x(g, mixed[g]))
         for g in range(PASSES):
-            turn_w(0, g, chunk, nc.scalar.copy)
-        quantise_x(PASSES - 1, grouped_before)
+            turn_w(0, g, chunks[0], nc.scalar.copy)
+        for g in range(GPSIMD_PASSES, PASSES):
+            regrouped.append(regroup_x(g, mixed[g]))
         for g in range(PASSES):
-            quantise_w(g, chunk)
+            quantise_x(g, regrouped[g])
+        for n in range(1, HEAD_CHUNKS):
+            for g in range(PASSES):
+                turn_w(n, g, chunks[n], nc.scalar.copy)
+        for g in range(PASSES):
+            quantise_w(g, chunks[0])
 
-        waiting = []
+        waiting = None
         for n in range(CHUNKS):
-            following = new_w_chunk() if n + 1 < CHUNKS else None
+            turn_next = HEAD_CHUNKS <= n + 1 < CHUNKS
+            if turn_next:
+                chunks.append(new_w_chunk())
             for first in range(0, B, STEP):
                 step = range(first, first + STEP)
-                if following is not None:
+                if turn_next:
                     for g in step:
                         last_copy = nc.vector.tensor_copy if g == step[-1] else nc.scalar.copy
-                        turn_w(n + 1, g, following, last_copy)
-                accs = [multiply(b, chunk) for b in step]
-                if following is not None:
+                        turn_w(n + 1, g, chunks[n + 1], last_copy)
+                accs = [multiply(b, chunks[n]) for b in step]
+                if n + 1 < CHUNKS:
                     for g in step:
-                        quantise_w(g, following)
-                scaled = [(n, b, times_gain(n, acc)) for b, acc in zip(step, accs)]
-                for tile_n, tile_b, kk in waiting:
-                    normalise_and_store(tile_n, tile_b, kk)
-                waiting = scaled
-            chunk = following
-        for tile_n, tile_b, kk in waiting:
-            normalise_and_store(tile_n, tile_b, kk)
+                        quantise_w(g, chunks[n + 1])
+                scaled = [(b, times_gain(n, acc)) for b, acc in zip(step, accs)]
+                if waiting is not None:
+                    normalise_and_store(waiting[0], waiting[1])
+                waiting = (n, scaled)
+        normalise_and_store(waiting[0], waiting[1])

@@ -251,8 +251,7 @@ def tile_full_tmix_params_pa_kernel(tc, x, x_k, Wk, k_k, out):
                 step = range(first, first + STEP)
                 if turn_next:
                     for g in step:
-                        last_copy = nc.vector.tensor_copy if g == step[-1] else nc.scalar.copy
-                        turn_w(n + 1, g, chunks[n + 1], last_copy)
+                        turn_w(n + 1, g, chunks[n + 1], nc.vector.tensor_copy)
                 accs = [multiply(b, chunks[n]) for b in step]
                 if n + 1 < CHUNKS:
                     for g in step:

@@ -46,15 +46,19 @@ def tile_full_tmix_params_pa_kernel(tc, x, x_k, Wk, k_k, out):
         turned = ctx.enter_context(tc.psum_pool(name="turned", bufs=4))
         sums = ctx.enter_context(tc.psum_pool(name="sums", bufs=4))
 
-        mix_bf = const.tile([P, PASSES * HALVES, PAIR], BF16)
-        with nc.allow_non_contiguous_dma(reason="x_k: 4 KiB, one word of two channels a piece"):
-            nc.scalar.dma_start(out=mix_bf[:], in_=x_k.rearrange("(a p e) -> p a e", p=P, e=PAIR))
+        mix_rows = const.tile([P, P * PAIR], BF16)
+        nc.vector.memset(mix_rows[:], 0.0)
         x_sb = [inputs.tile([P, B, K_PASS], BF16, name="x_sb%d" % g) for g in range(PASSES)]
         for g in range(PASSES):
             nc.sync.dma_start(
                 out=x_sb[g][:],
                 in_=x[:, :, g * K_PASS : (g + 1) * K_PASS].rearrange("b s k -> s b k"),
             )
+            if g == 0:
+                nc.sync.dma_start(
+                    out=mix_rows[0 : PASSES * HALVES, :],
+                    in_=x_k.rearrange("(a w) -> a w", w=P * PAIR),
+                )
         w_sb = [inputs.tile([P, C], BF16, name="w_sb%d" % r) for r in range(C // P)]
         gain = const.tile([P, C], BF16)
         for r in range(C // P):
@@ -71,10 +75,12 @@ def tile_full_tmix_params_pa_kernel(tc, x, x_k, Wk, k_k, out):
             const.tile([P, PAIR, B, T + 1], F32, name="prev_term%d" % i) for i in range(PASSES)
         ]
         for i in range(PASSES):
-            nc.vector.memset(prev_term[i][:], 0.0)
+            nc.vector.memset(prev_term[i][:, :, :, 0:1], 0.0)
         mix = const.tile([P, PASSES * PACK], F32)
         keep = const.tile([P, PASSES * PACK], F32)
-        nc.vector.tensor_copy(out=mix[:], in_=mix_bf[:].rearrange("p a e -> p (a e)"))
+        mix_turned = turned.tile([P, P], F32, name="mix_turned", tag="bank")
+        nc.tensor.transpose(mix_turned[:], mix_rows[:].bitcast(F32), ident[:])
+        nc.vector.tensor_copy(out=mix[:], in_=mix_turned[:].bitcast(BF16)[:, 0 : PASSES * PACK])
         nc.vector.tensor_scalar(
             out=keep[:], in0=mix[:], scalar1=-1.0, scalar2=1.0, op0=ALU.mult, op1=ALU.add
         )

@@ -41,24 +41,37 @@ def tile_full_tmix_params_pa_kernel(tc, x, x_k, Wk, k_k, out):
         inputs = ctx.enter_context(tc.tile_pool(name="inputs", bufs=1))
         x_work = ctx.enter_context(tc.tile_pool(name="x_work", bufs=PASSES))
         w_work = ctx.enter_context(tc.tile_pool(name="w_work", bufs=2))
-        results = ctx.enter_context(tc.tile_pool(name="results", bufs=8))
+        results = ctx.enter_context(tc.tile_pool(name="results", bufs=12))
         scratch = ctx.enter_context(tc.tile_pool(name="scratch", bufs=2))
+        small = ctx.enter_context(tc.tile_pool(name="small", bufs=8))
         turned = ctx.enter_context(tc.psum_pool(name="turned", bufs=4))
         sums = ctx.enter_context(tc.psum_pool(name="sums", bufs=4))
 
-        mix_rows = const.tile([P, P * PAIR], BF16)
-        nc.vector.memset(mix_rows[:], 0.0)
-        x_sb = [inputs.tile([P, B, K_PASS], BF16, name="x_sb%d" % g) for g in range(PASSES)]
-        for g in range(PASSES):
+        mix_bf = const.tile([P, PASSES * HALVES, PAIR], BF16)
+        x_first = [inputs.tile([P, B, PAIR * P], BF16, name="x_first%d" % u) for u in range(HALVES)]
+        x_rest = [inputs.tile([P, B, K_PASS], BF16, name="x_rest%d" % g) for g in range(1, PASSES)]
+
+        def load_x(tile, seqs, first_k):
             nc.sync.dma_start(
-                out=x_sb[g][:],
-                in_=x[:, :, g * K_PASS : (g + 1) * K_PASS].rearrange("b s k -> s b k"),
+                out=tile,
+                in_=x[seqs, :, first_k : first_k + tile.shape[2]].rearrange("b s k -> s b k"),
             )
+
+        for half in (slice(0, B // 2), slice(B // 2, B)):
+            load_x(x_first[0][:, half, :], half, 0)
+            if half.start == 0:
+                with nc.allow_non_contiguous_dma(reason="x_k: 4 KiB, one word of two channels a piece"):
+                    nc.sync.dma_start(out=mix_bf[:], in_=x_k.rearrange("(a p e) -> p a e", p=P, e=PAIR))
+        load_x(x_first[1][:], slice(0, B), PAIR * P)
+        for g in range(1, PASSES):
+            load_x(x_rest[g - 1][:], slice(0, B), g * K_PASS)
+
+        def x_words(a, b):
+            g, u = divmod(a, HALVES)
             if g == 0:
-                nc.sync.dma_start(
-                    out=mix_rows[0 : PASSES * HALVES, :],
-                    in_=x_k.rearrange("(a w) -> a w", w=P * PAIR),
-                )
+                return x_first[u][:, b, :].bitcast(F32)
+            return x_rest[g - 1][:, b, u * PAIR * P : (u + 1) * PAIR * P].bitcast(F32)
+
         w_sb = [inputs.tile([P, C], BF16, name="w_sb%d" % r) for r in range(C // P)]
         gain = const.tile([P, C], BF16)
         for r in range(C // P):
@@ -78,9 +91,7 @@ def tile_full_tmix_params_pa_kernel(tc, x, x_k, Wk, k_k, out):
             nc.vector.memset(prev_term[i][:, :, :, 0:1], 0.0)
         mix = const.tile([P, PASSES * PACK], F32)
         keep = const.tile([P, PASSES * PACK], F32)
-        mix_turned = turned.tile([P, P], F32, name="mix_turned", tag="bank")
-        nc.tensor.transpose(mix_turned[:], mix_rows[:].bitcast(F32), ident[:])
-        nc.vector.tensor_copy(out=mix[:], in_=mix_turned[:].bitcast(BF16)[:, 0 : PASSES * PACK])
+        nc.vector.tensor_copy(out=mix[:], in_=mix_bf[:].rearrange("p a e -> p (a e)"))
         nc.vector.tensor_scalar(
             out=keep[:], in0=mix[:], scalar1=-1.0, scalar2=1.0, op0=ALU.mult, op1=ALU.add
         )
@@ -88,40 +99,48 @@ def tile_full_tmix_params_pa_kernel(tc, x, x_k, Wk, k_k, out):
         x_codes = const.tile([P, PASSES, B * T], U32, align_bytes=64)
         x_scales = const.tile([P, PASSES, B * T], U8, align_bytes=64)
 
-        x_turned = []
-        for a in range(PASSES * HALVES):
-            pool = turned if a % HALVES == 0 else sums
-            bank = pool.tile([P, B, T], F32, name="x_turned", tag="bank")
-            for b in range(B):
-                words = x_sb[a // HALVES][:, b, :].bitcast(F32)
-                u = a % HALVES
-                nc.tensor.transpose(bank[:, b, :], words[:, u * P : (u + 1) * P], ident[:])
-            x_turned.append(bank)
+        x_turned = {}
+
+        def turn_x(a):
+            g, u = divmod(a, HALVES)
+            ends = a in (0, PASSES * HALVES - 1)
+            parts = [range(0, B // 2), range(B // 2, B)] if ends else [range(B)]
+            x_turned[a] = []
+            for seqs in parts:
+                pool = turned if u == 0 else sums
+                bank = pool.tile([P, len(seqs), T], F32, name="x_turned", tag="bank")
+                for i, b in enumerate(seqs):
+                    nc.tensor.transpose(bank[:, i, :], x_words(a, b), ident[:])
+                x_turned[a].append((seqs, bank))
 
         def mix_x(g):
             planes = x_work.tile([P, PACK, B * T], BF16)
             for u in range(HALVES):
                 a = HALVES * g + u
-                x_halves = x_turned[a][:].bitcast(BF16).rearrange("p b (s e) -> p b s e", e=PAIR)
                 shifted = prev_term[a % PASSES]
-                for e in range(PAIR):
-                    col = PAIR * a + e
-                    nc.scalar.activation(
-                        out=shifted[:, e, :, 1 : T + 1],
-                        in_=x_halves[:, :, :, e],
-                        func=ACT.Copy,
-                        scale=mix[:, col : col + 1],
-                    )
-                for e in range(PAIR):
-                    col = PAIR * a + e
-                    nc.vector.scalar_tensor_tensor(
-                        out=planes[:, PAIR * u + e, :].rearrange("p (b s) -> p b s", b=B),
-                        in0=x_halves[:, :, :, e],
-                        scalar=keep[:, col : col + 1],
-                        in1=shifted[:, e, :, 0:T],
-                        op0=ALU.mult,
-                        op1=ALU.add,
-                    )
+                for seqs, bank in x_turned[a]:
+                    x_halves = bank[:].bitcast(BF16).rearrange("p b (s e) -> p b s e", e=PAIR)
+                    now = slice(seqs.start, seqs.stop)
+                    for e in range(PAIR):
+                        col = PAIR * a + e
+                        nc.scalar.activation(
+                            out=shifted[:, e, now, 1 : T + 1],
+                            in_=x_halves[:, :, :, e],
+                            func=ACT.Copy,
+                            scale=mix[:, col : col + 1],
+                        )
+                    for e in range(PAIR):
+                        col = PAIR * a + e
+                        nc.vector.scalar_tensor_tensor(
+                            out=planes[:, PAIR * u + e, now.start * T : now.stop * T].rearrange(
+                                "p (b s) -> p b s", b=len(seqs)
+                            ),
+                            in0=x_halves[:, :, :, e],
+                            scalar=keep[:, col : col + 1],
+                            in1=shifted[:, e, now, 0:T],
+                            op0=ALU.mult,
+                            op1=ALU.add,
+                        )
             return planes
 
         def regroup_x(g, planes):
@@ -178,19 +197,22 @@ def tile_full_tmix_params_pa_kernel(tc, x, x_k, Wk, k_k, out):
                 in_=chunk["grouped"][:, g, :, :].rearrange("p c t -> p (c t)"),
             )
 
-        def multiply(b, chunk):
+        def multiply_pass(b, g, chunk, acc):
             toks = slice(b * T, (b + 1) * T)
+            nc.tensor.matmul_mx(
+                out=acc[:],
+                lhsT=x_codes[:, g, toks].bitcast(FP8X4),
+                lhsT_scale=x_scales[:, g, toks],
+                rhs=chunk["codes"][:, g, :].bitcast(FP8X4),
+                rhs_scale=chunk["scales"][:, g, :],
+                start=(g == 0),
+                stop=(g == PASSES - 1),
+            )
+
+        def multiply(b, chunk):
             acc = sums.tile([P, N_CHUNK], F32, name="acc", tag="bank")
             for g in range(PASSES):
-                nc.tensor.matmul_mx(
-                    out=acc[:],
-                    lhsT=x_codes[:, g, toks].bitcast(FP8X4),
-                    lhsT_scale=x_scales[:, g, toks],
-                    rhs=chunk["codes"][:, g, :].bitcast(FP8X4),
-                    rhs_scale=chunk["scales"][:, g, :],
-                    start=(g == 0),
-                    stop=(g == PASSES - 1),
-                )
+                multiply_pass(b, g, chunk, acc)
             return acc
 
         def times_gain(n, acc):
@@ -203,53 +225,120 @@ def tile_full_tmix_params_pa_kernel(tc, x, x_k, Wk, k_k, out):
             )
             return kk
 
-        def normalise_and_store(n, tiles):
+        def square_heads(tiles):
             squares = scratch.tile([P, STEP, HEADS, HEAD], F32)
-            sumsq = scratch.tile([P, STEP, HEADS], F32)
+            sumsq = small.tile([P, STEP, HEADS], F32)
             for i, (b, kk) in enumerate(tiles):
                 for h in range(HEADS):
                     nc.scalar.activation(
                         out=squares[:, i, h, :], in_=kk[:, h, :], func=ACT.Square,
                         accum_out=sumsq[:, i, h : h + 1],
                     )
-            inverse = scratch.tile([P, STEP, HEADS], F32)
-            nc.scalar.activation(out=inverse[:], in_=sumsq[:], func=ACT.Abs_reciprocal_sqrt)
-            capped = scratch.tile([P, STEP, HEADS], F32)
-            nc.vector.tensor_scalar_min(out=capped[:], in0=inverse[:], scalar1=1e12)
-            engine = nc.gpsimd if n + 1 < CHUNKS else nc.vector
+            return sumsq
+
+        def invert(tiles, sumsq):
+            used = slice(0, len(tiles))
+            inverse = small.tile([P, STEP, HEADS], F32)
+            nc.scalar.activation(
+                out=inverse[:, used, :], in_=sumsq[:, used, :], func=ACT.Abs_reciprocal_sqrt
+            )
+            return inverse
+
+        def head_statistics(kk):
+            stats = small.tile([P, HEADS // 2, 2, 3], F32, name="stats")
+            for h in range(0, HEADS, 2):
+                nc.vector.bn_stats(
+                    out=stats[:, h // 2, :, :].rearrange("p a s -> p (a s)"),
+                    in_=kk[:, h : h + 2, :].rearrange("p a d -> p d a"),
+                )
+            return stats
+
+        def squares_from(stats):
+            mean = stats[:, :, :, 1].rearrange("p h a -> p (h a)")
+            spread = stats[:, :, :, 2].rearrange("p h a -> p (h a)")
+            mean_part = small.tile([P, HEADS], F32, name="mean_part")
+            nc.vector.scalar_tensor_tensor(
+                out=mean_part[:], in0=mean, scalar=float(HEAD), in1=mean, op0=ALU.mult, op1=ALU.mult
+            )
+            sumsq = small.tile([P, STEP, HEADS], F32, name="sumsq")
+            nc.vector.tensor_tensor(out=sumsq[:, 0, :], in0=mean_part[:], in1=spread, op=ALU.add)
+            return sumsq
+
+        def store(n, b, kk):
+            nc.sync.dma_start(
+                out=out[b, :, n * N_CHUNK : (n + 1) * N_CHUNK],
+                in_=kk[:].rearrange("p h d -> p (h d)"),
+            )
+
+        def scale_and_store(n, tiles, inverse, engine, offset=0, later=False):
+            if engine is nc.gpsimd:
+                capped = small.tile([P, STEP, HEADS], F32)
+                nc.gpsimd.tensor_scalar(
+                    out=capped[:], in0=inverse[:], scalar1=1e12, scalar2=0.0, op0=ALU.min, op1=ALU.add
+                )
             for i, (b, kk) in enumerate(tiles):
-                engine.tensor_tensor(
-                    out=kk[:],
-                    in0=kk[:],
-                    in1=capped[:, i, :].unsqueeze(2).to_broadcast([P, HEADS, HEAD]),
-                    op=ALU.mult,
-                )
-                nc.sync.dma_start(
-                    out=out[b, :, n * N_CHUNK : (n + 1) * N_CHUNK],
-                    in_=kk[:].rearrange("p h d -> p (h d)"),
-                )
+                i += offset
+                if engine is nc.gpsimd:
+                    nc.gpsimd.tensor_tensor(
+                        out=kk[:],
+                        in0=kk[:],
+                        in1=capped[:, i, :].unsqueeze(2).to_broadcast([P, HEADS, HEAD]),
+                        op=ALU.mult,
+                    )
+                else:
+                    nc.vector.scalar_tensor_tensor(
+                        out=kk[:],
+                        in0=inverse[:, i, :].unsqueeze(2).to_broadcast([P, HEADS, HEAD]),
+                        scalar=1e12,
+                        in1=kk[:],
+                        op0=ALU.min,
+                        op1=ALU.mult,
+                    )
+                if engine is nc.gpsimd and not later:
+                    store(n, b, kk)
+                elif engine is nc.vector:
+                    store(n, b, kk)
 
         chunks = [new_w_chunk() for n in range(HEAD_CHUNKS)]
         mixed = []
         regrouped = []
+        for a in range((PASSES - 1) * HALVES):
+            turn_x(a)
         for g in range(PASSES):
             mixed.append(mix_x(g))
             if g < GPSIMD_PASSES:
                 regrouped.append(regroup_x(g, mixed[g]))
+            if g == 0:
+                for a in range((PASSES - 1) * HALVES, PASSES * HALVES):
+                    turn_x(a)
         for g in range(PASSES):
             turn_w(0, g, chunks[0], nc.scalar.copy)
-        for g in range(GPSIMD_PASSES, PASSES):
-            regrouped.append(regroup_x(g, mixed[g]))
-        for g in range(PASSES):
-            quantise_x(g, regrouped[g])
-        for n in range(1, HEAD_CHUNKS):
-            for g in range(PASSES):
-                turn_w(n, g, chunks[n], nc.scalar.copy)
-        for g in range(PASSES):
-            quantise_w(g, chunks[0])
+        first_accs = [sums.tile([P, N_CHUNK], F32, name="acc", tag="bank") for b in range(B)]
+
+        def first_pass(g):
+            if g >= GPSIMD_PASSES:
+                regrouped.append(regroup_x(g, mixed[g]))
+            if g < GPSIMD_PASSES:
+                quantise_x(g, regrouped[g])
+                quantise_w(g, chunks[0])
+            else:
+                quantise_w(g, chunks[0])
+                quantise_x(g, regrouped[g])
+            for b in range(B):
+                multiply_pass(b, g, chunks[0], first_accs[b])
+
+        turn_w(1, 0, chunks[1], nc.scalar.copy)
+        first_pass(0)
+        turn_w(1, 1, chunks[1], nc.scalar.copy)
+        first_pass(1)
+        turn_w(1, 2, chunks[1], nc.scalar.copy)
+        turn_w(1, 3, chunks[1], nc.scalar.copy)
+        first_pass(2)
+        first_pass(3)
 
         waiting = None
-        for n in range(CHUNKS):
+        squared = None
+        for n in range(CHUNKS - 1):
             turn_next = HEAD_CHUNKS <= n + 1 < CHUNKS
             if turn_next:
                 chunks.append(new_w_chunk())
@@ -257,13 +346,43 @@ def tile_full_tmix_params_pa_kernel(tc, x, x_k, Wk, k_k, out):
                 step = range(first, first + STEP)
                 if turn_next:
                     for g in step:
-                        turn_w(n + 1, g, chunks[n + 1], nc.vector.tensor_copy)
-                accs = [multiply(b, chunks[n]) for b in step]
-                if n + 1 < CHUNKS:
-                    for g in step:
-                        quantise_w(g, chunks[n + 1])
+                        turn_w(n + 1, g, chunks[n + 1], nc.scalar.copy if (n == 2 and first == 2) else nc.vector.tensor_copy)
+                accs = [first_accs[b] if n == 0 else multiply(b, chunks[n]) for b in step]
+                for g in step:
+                    quantise_w(g, chunks[n + 1])
                 scaled = [(b, times_gain(n, acc)) for b, acc in zip(step, accs)]
+                if squared is not None:
+                    m, tiles, sumsq = squared
+                    scale_and_store(m, tiles, invert(tiles, sumsq), nc.gpsimd)
+                    squared = None
                 if waiting is not None:
-                    normalise_and_store(waiting[0], waiting[1])
+                    squared = (waiting[0], waiting[1], square_heads(waiting[1]))
                 waiting = (n, scaled)
-        normalise_and_store(waiting[0], waiting[1])
+        n = CHUNKS - 1
+        accs = [multiply(0, chunks[n]), multiply(1, chunks[n])]
+        kks = [times_gain(n, accs[0])]
+        m, tiles, sumsq = squared
+        scale_and_store(m, tiles, invert(tiles, sumsq), nc.gpsimd)
+        late = waiting[1]
+        sumsq = square_heads(late)
+        inverse = invert(late, sumsq)
+        scale_and_store(waiting[0], late[:1], inverse, nc.gpsimd, later=True)
+        accs += [multiply(2, chunks[n]), multiply(3, chunks[n])]
+        stats = head_statistics(kks[0])
+        kks.append(times_gain(n, accs[1]))
+        sums0 = squares_from(stats)
+        kks.append(times_gain(n, accs[2]))
+        sums1 = square_heads([(1, kks[1])])
+        scale_and_store(waiting[0], late[1:], inverse, nc.vector, 1)
+        inv0 = invert([0], sums0)
+        kks.append(times_gain(n, accs[3]))
+        sums2 = square_heads([(2, kks[2])])
+        inv1 = invert([0], sums1)
+        scale_and_store(n, [(0, kks[0])], inv0, nc.vector)
+        scale_and_store(n, [(1, kks[1])], inv1, nc.vector)
+        store(waiting[0], late[0][0], late[0][1])
+        sums3 = square_heads([(3, kks[3])])
+        inv2 = invert([0], sums2)
+        scale_and_store(n, [(2, kks[2])], inv2, nc.vector)
+        inv3 = invert([0], sums3)
+        scale_and_store(n, [(3, kks[3])], inv3, nc.vector)

@@ -47,7 +47,8 @@ def tile_full_tmix_params_pa_kernel(tc, x, x_k, Wk, k_k, out):
         turned = ctx.enter_context(tc.psum_pool(name="turned", bufs=4))
         sums = ctx.enter_context(tc.psum_pool(name="sums", bufs=4))
 
-        mix_bf = const.tile([P, PASSES * HALVES, PAIR], BF16)
+        mix_rows = const.tile([P, P * PAIR], BF16)
+        nc.vector.memset(mix_rows[:], 0.0)
         x_first = [inputs.tile([P, B, PAIR * P], BF16, name="x_first%d" % u) for u in range(HALVES)]
         x_rest = [inputs.tile([P, B, K_PASS], BF16, name="x_rest%d" % g) for g in range(1, PASSES)]
 
@@ -60,8 +61,9 @@ def tile_full_tmix_params_pa_kernel(tc, x, x_k, Wk, k_k, out):
         for half in (slice(0, B // 2), slice(B // 2, B)):
             load_x(x_first[0][:, half, :], half, 0)
             if half.start == 0:
-                with nc.allow_non_contiguous_dma(reason="x_k: 4 KiB, one word of two channels a piece"):
-                    nc.sync.dma_start(out=mix_bf[:], in_=x_k.rearrange("(a p e) -> p a e", p=P, e=PAIR))
+                nc.sync.dma_start(
+                    out=mix_rows[0 : PASSES * HALVES, :], in_=x_k.rearrange("(a w) -> a w", w=P * PAIR)
+                )
         load_x(x_first[1][:], slice(0, B), PAIR * P)
         for g in range(1, PASSES):
             load_x(x_rest[g - 1][:], slice(0, B), g * K_PASS)
@@ -91,7 +93,9 @@ def tile_full_tmix_params_pa_kernel(tc, x, x_k, Wk, k_k, out):
             nc.vector.memset(prev_term[i][:, :, :, 0:1], 0.0)
         mix = const.tile([P, PASSES * PACK], F32)
         keep = const.tile([P, PASSES * PACK], F32)
-        nc.vector.tensor_copy(out=mix[:], in_=mix_bf[:].rearrange("p a e -> p (a e)"))
+        mix_turned = turned.tile([P, P], F32, name="mix_turned", tag="bank")
+        nc.tensor.transpose(mix_turned[:], mix_rows[:].bitcast(F32), ident[:])
+        nc.vector.tensor_copy(out=mix[:], in_=mix_turned[:].bitcast(BF16)[:, 0 : PASSES * PACK])
         nc.vector.tensor_scalar(
             out=keep[:], in0=mix[:], scalar1=-1.0, scalar2=1.0, op0=ALU.mult, op1=ALU.add
         )

@@ -277,9 +277,12 @@ def tile_full_tmix_params_pa_kernel(tc, x, x_k, Wk, k_k, out):
         def scale_and_store(n, tiles, inverse, engine, offset=0, later=False):
             if engine is nc.gpsimd:
                 capped = small.tile([P, STEP, HEADS], F32)
-                nc.gpsimd.tensor_scalar(
-                    out=capped[:], in0=inverse[:], scalar1=1e12, scalar2=0.0, op0=ALU.min, op1=ALU.add
-                )
+                if later:
+                    nc.gpsimd.tensor_scalar(
+                        out=capped[:], in0=inverse[:], scalar1=1e12, scalar2=0.0, op0=ALU.min, op1=ALU.add
+                    )
+                else:
+                    nc.vector.tensor_scalar_min(out=capped[:], in0=inverse[:], scalar1=1e12)
             for i, (b, kk) in enumerate(tiles):
                 i += offset
                 if engine is nc.gpsimd:
@@ -354,19 +357,19 @@ def tile_full_tmix_params_pa_kernel(tc, x, x_k, Wk, k_k, out):
                 accs = [first_accs[b] if n == 0 else multiply(b, chunks[n]) for b in step]
                 for g in step:
                     quantise_w(g, chunks[n + 1])
-                scaled = [(b, times_gain(n, acc)) for b, acc in zip(step, accs)]
                 if squared is not None:
                     m, tiles, sumsq = squared
                     scale_and_store(m, tiles, invert(tiles, sumsq), nc.gpsimd)
                     squared = None
+                scaled = [(b, times_gain(n, acc)) for b, acc in zip(step, accs)]
                 if waiting is not None:
                     squared = (waiting[0], waiting[1], square_heads(waiting[1]))
                 waiting = (n, scaled)
         n = CHUNKS - 1
         accs = [multiply(0, chunks[n]), multiply(1, chunks[n])]
-        kks = [times_gain(n, accs[0])]
         m, tiles, sumsq = squared
         scale_and_store(m, tiles, invert(tiles, sumsq), nc.gpsimd)
+        kks = [times_gain(n, accs[0])]
         late = waiting[1]
         sumsq = square_heads(late)
         inverse = invert(late, sumsq)

@@ -41,9 +41,9 @@ def tile_full_tmix_params_pa_kernel(tc, x, x_k, Wk, k_k, out):
         inputs = ctx.enter_context(tc.tile_pool(name="inputs", bufs=1))
         x_work = ctx.enter_context(tc.tile_pool(name="x_work", bufs=PASSES))
         w_work = ctx.enter_context(tc.tile_pool(name="w_work", bufs=2))
-        results = ctx.enter_context(tc.tile_pool(name="results", bufs=12))
+        results = ctx.enter_context(tc.tile_pool(name="results", bufs=14))
         scratch = ctx.enter_context(tc.tile_pool(name="scratch", bufs=2))
-        small = ctx.enter_context(tc.tile_pool(name="small", bufs=8))
+        small = ctx.enter_context(tc.tile_pool(name="small", bufs=10))
         turned = ctx.enter_context(tc.psum_pool(name="turned", bufs=4))
         sums = ctx.enter_context(tc.psum_pool(name="sums", bufs=4))
 
@@ -248,63 +248,43 @@ def tile_full_tmix_params_pa_kernel(tc, x, x_k, Wk, k_k, out):
             )
             return inverse
 
-        def head_statistics(kk):
-            stats = small.tile([P, HEADS // 2, 2, 3], F32, name="stats")
-            for h in range(0, HEADS, 2):
-                nc.vector.bn_stats(
-                    out=stats[:, h // 2, :, :].rearrange("p a s -> p (a s)"),
-                    in_=kk[:, h : h + 2, :].rearrange("p a d -> p d a"),
-                )
-            return stats
-
-        def squares_from(stats):
-            mean = stats[:, :, :, 1].rearrange("p h a -> p (h a)")
-            spread = stats[:, :, :, 2].rearrange("p h a -> p (h a)")
-            mean_part = small.tile([P, HEADS], F32, name="mean_part")
-            nc.vector.scalar_tensor_tensor(
-                out=mean_part[:], in0=mean, scalar=float(HEAD), in1=mean, op0=ALU.mult, op1=ALU.mult
-            )
-            sumsq = small.tile([P, STEP, HEADS], F32, name="sumsq")
-            nc.vector.tensor_tensor(out=sumsq[:, 0, :], in0=mean_part[:], in1=spread, op=ALU.add)
-            return sumsq
-
         def store(n, b, kk):
             nc.sync.dma_start(
                 out=out[b, :, n * N_CHUNK : (n + 1) * N_CHUNK],
                 in_=kk[:].rearrange("p h d -> p (h d)"),
             )
 
-        def scale_and_store(n, tiles, inverse, engine, offset=0, later=False):
-            if engine is nc.gpsimd:
-                capped = small.tile([P, STEP, HEADS], F32)
-                if later:
-                    nc.gpsimd.tensor_scalar(
-                        out=capped[:], in0=inverse[:], scalar1=1e12, scalar2=0.0, op0=ALU.min, op1=ALU.add
-                    )
-                else:
-                    nc.vector.tensor_scalar_min(out=capped[:], in0=inverse[:], scalar1=1e12)
-            for i, (b, kk) in enumerate(tiles):
-                i += offset
-                if engine is nc.gpsimd:
-                    nc.gpsimd.tensor_tensor(
-                        out=kk[:],
-                        in0=kk[:],
-                        in1=capped[:, i, :].unsqueeze(2).to_broadcast([P, HEADS, HEAD]),
-                        op=ALU.mult,
-                    )
-                else:
-                    nc.vector.scalar_tensor_tensor(
-                        out=kk[:],
-                        in0=inverse[:, i, :].unsqueeze(2).to_broadcast([P, HEADS, HEAD]),
-                        scalar=1e12,
-                        in1=kk[:],
-                        op0=ALU.min,
-                        op1=ALU.mult,
-                    )
-                if engine is nc.gpsimd and not later:
-                    store(n, b, kk)
-                elif engine is nc.vector:
-                    store(n, b, kk)
+        def cap(inverse):
+            capped = small.tile([P, STEP, HEADS], F32)
+            nc.vector.tensor_scalar_min(out=capped[:], in0=inverse[:], scalar1=1e12)
+            return capped
+
+        def scale_on_gpsimd(n, b, kk, capped, i):
+            nc.gpsimd.tensor_tensor(
+                out=kk[:],
+                in0=kk[:],
+                in1=capped[:, i, :].unsqueeze(2).to_broadcast([P, HEADS, HEAD]),
+                op=ALU.mult,
+            )
+            store(n, b, kk)
+
+        def scale_on_scalar(n, b, kk, capped, i):
+            for h in range(HEADS):
+                nc.scalar.activation(
+                    out=kk[:, h, :], in_=kk[:, h, :], func=ACT.Copy, scale=capped[:, i, h : h + 1]
+                )
+            store(n, b, kk)
+
+        def scale_on_vector(n, b, kk, inverse, i):
+            nc.vector.scalar_tensor_tensor(
+                out=kk[:],
+                in0=inverse[:, i, :].unsqueeze(2).to_broadcast([P, HEADS, HEAD]),
+                scalar=1e12,
+                in1=kk[:],
+                op0=ALU.min,
+                op1=ALU.mult,
+            )
+            store(n, b, kk)
 
         chunks = [new_w_chunk() for n in range(HEAD_CHUNKS)]
         mixed = []
@@ -318,12 +298,10 @@ def tile_full_tmix_params_pa_kernel(tc, x, x_k, Wk, k_k, out):
             if g == 0:
                 for a in range((PASSES - 1) * HALVES, PASSES * HALVES):
                     turn_x(a)
-        for g in range(PASSES):
-            turn_w(0, g, chunks[0], nc.scalar.copy)
-        first_accs = [sums.tile([P, N_CHUNK], F32, name="acc", tag="bank") for b in range(B)]
+        first_accs = []
 
         def first_pass(g):
-            if g >= GPSIMD_PASSES:
+            if g >= GPSIMD_PASSES and len(regrouped) == g:
                 regrouped.append(regroup_x(g, mixed[g]))
             if g < GPSIMD_PASSES:
                 quantise_x(g, regrouped[g])
@@ -331,20 +309,29 @@ def tile_full_tmix_params_pa_kernel(tc, x, x_k, Wk, k_k, out):
             else:
                 quantise_w(g, chunks[0])
                 quantise_x(g, regrouped[g])
+            if g == 0:
+                for b in range(B):
+                    acc = sums.tile([P, N_CHUNK], F32, name="acc", tag="bank")
+                    first_accs.append(acc)
             for b in range(B):
                 multiply_pass(b, g, chunks[0], first_accs[b])
 
-        turn_w(1, 0, chunks[1], nc.scalar.copy)
+        turn_w(0, 0, chunks[0], nc.scalar.copy)
+        turn_w(0, 1, chunks[0], nc.scalar.copy)
+        turn_w(0, 2, chunks[0], nc.scalar.copy)
+        turn_w(0, 3, chunks[0], nc.scalar.copy)
         first_pass(0)
-        turn_w(1, 1, chunks[1], nc.scalar.copy)
+        turn_w(1, 0, chunks[1], nc.scalar.copy)
         first_pass(1)
+        turn_w(1, 1, chunks[1], nc.scalar.copy)
+        first_pass(2)
         turn_w(1, 2, chunks[1], nc.scalar.copy)
         turn_w(1, 3, chunks[1], nc.scalar.copy)
-        first_pass(2)
         first_pass(3)
 
         waiting = None
         squared = None
+        late = None
         for n in range(CHUNKS - 1):
             turn_next = HEAD_CHUNKS <= n + 1 < CHUNKS
             if turn_next:
@@ -353,43 +340,55 @@ def tile_full_tmix_params_pa_kernel(tc, x, x_k, Wk, k_k, out):
                 step = range(first, first + STEP)
                 if turn_next:
                     for g in step:
-                        turn_w(n + 1, g, chunks[n + 1], nc.scalar.copy if (n == 2 and first == 2) else nc.vector.tensor_copy)
+                        turn_w(n + 1, g, chunks[n + 1], nc.scalar.copy if False else nc.vector.tensor_copy)
                 accs = [first_accs[b] if n == 0 else multiply(b, chunks[n]) for b in step]
+                if squared is not None:
+                    inverse = invert(squared[1], squared[2])
+                if late is not None:
+                    scale_on_scalar(*late)
+                    late = None
+                tiles = None
+                if waiting is not None:
+                    m, seqs, sums_of = waiting
+                    tiles = [(b, times_gain(m, acc)) for b, acc in zip(seqs, sums_of)]
+                    sumsq = square_heads(tiles)
                 for g in step:
                     quantise_w(g, chunks[n + 1])
                 if squared is not None:
-                    m, tiles, sumsq = squared
-                    scale_and_store(m, tiles, invert(tiles, sumsq), nc.gpsimd)
-                    squared = None
-                scaled = [(b, times_gain(n, acc)) for b, acc in zip(step, accs)]
-                if waiting is not None:
-                    squared = (waiting[0], waiting[1], square_heads(waiting[1]))
-                waiting = (n, scaled)
+                    capped = cap(inverse)
+                    (b0, kk0), (b1, kk1) = squared[1]
+                    scale_on_gpsimd(squared[0], b0, kk0, capped, 0)
+                    late = (squared[0], b1, kk1, capped, 1)
+                squared = None if tiles is None else (m, tiles, sumsq)
+                waiting = (n, step, accs)
         n = CHUNKS - 1
-        accs = [multiply(0, chunks[n]), multiply(1, chunks[n])]
-        m, tiles, sumsq = squared
-        scale_and_store(m, tiles, invert(tiles, sumsq), nc.gpsimd)
+        m, seqs, sums_of = waiting
+        accs = [multiply(b, chunks[n]) for b in range(STEP)]
+        inverse = invert(squared[1], squared[2])
+        if late is not None:
+            scale_on_scalar(*late)
+        last = [(b, times_gain(m, acc)) for b, acc in zip(seqs, sums_of)]
+        accs += [multiply(b, chunks[n]) for b in range(STEP, B)]
+        (b0, kk0), (b1, kk1) = squared[1]
+        sumsq = square_heads(last)
         kks = [times_gain(n, accs[0])]
-        late = waiting[1]
-        sumsq = square_heads(late)
-        inverse = invert(late, sumsq)
-        scale_and_store(waiting[0], late[:1], inverse, nc.gpsimd, later=True)
-        accs += [multiply(2, chunks[n]), multiply(3, chunks[n])]
-        stats = head_statistics(kks[0])
+        scale_on_vector(squared[0], b0, kk0, inverse, 0)
         kks.append(times_gain(n, accs[1]))
-        sums0 = squares_from(stats)
+        scale_on_vector(squared[0], b1, kk1, inverse, 1)
+        inverse = invert(last, sumsq)
+        sums0 = square_heads([(0, kks[0])])
         kks.append(times_gain(n, accs[2]))
+        scale_on_vector(m, last[0][0], last[0][1], inverse, 0)
         sums1 = square_heads([(1, kks[1])])
-        scale_and_store(waiting[0], late[1:], inverse, nc.vector, 1)
         inv0 = invert([0], sums0)
         kks.append(times_gain(n, accs[3]))
+        scale_on_vector(m, last[1][0], last[1][1], inverse, 1)
         sums2 = square_heads([(2, kks[2])])
         inv1 = invert([0], sums1)
-        scale_and_store(n, [(0, kks[0])], inv0, nc.vector)
-        scale_and_store(n, [(1, kks[1])], inv1, nc.vector)
-        store(waiting[0], late[0][0], late[0][1])
+        scale_on_vector(n, 0, kks[0], inv0, 0)
+        scale_on_vector(n, 1, kks[1], inv1, 0)
         sums3 = square_heads([(3, kks[3])])
         inv2 = invert([0], sums2)
-        scale_and_store(n, [(2, kks[2])], inv2, nc.vector)
+        scale_on_vector(n, 2, kks[2], inv2, 0)
         inv3 = invert([0], sums3)
-        scale_and_store(n, [(3, kks[3])], inv3, nc.vector)
+        scale_on_vector(n, 3, kks[3], inv3, 0)

from contextlib import ExitStack

import concourse.mybir as mybir
from concourse.masks import make_identity

F32 = mybir.dt.float32
BF16 = mybir.dt.bfloat16
U32 = mybir.dt.uint32
U8 = mybir.dt.uint8
FP8X4 = mybir.dt.float8_e4m3fn_x4
ACT = mybir.ActivationFunctionType
ALU = mybir.AluOpType

P = 128
B = 4
T = 128
C = 2048
HEAD = 64
PACK = 4
PAIR = 2
HALVES = PACK // PAIR
K_PASS = P * PACK
PASSES = C // K_PASS
N_CHUNK = 512
CHUNKS = C // N_CHUNK
ROW_TILES = N_CHUNK // P
HEADS = N_CHUNK // HEAD
BANK_TILES = 2
STEP = 2
HEAD_CHUNKS = 2
GPSIMD_PASSES = 2

FLOPS = 2 * B * T * C * C


def tile_full_tmix_params_pa_kernel(tc, x, x_k, Wk, k_k, out):
    nc = tc.nc
    with ExitStack() as ctx:
        ctx.enter_context(tc.manual_schedule())
        const = ctx.enter_context(tc.tile_pool(name="const", bufs=1))
        inputs = ctx.enter_context(tc.tile_pool(name="inputs", bufs=1))
        x_work = ctx.enter_context(tc.tile_pool(name="x_work", bufs=PASSES))
        w_work = ctx.enter_context(tc.tile_pool(name="w_work", bufs=2))
        results = ctx.enter_context(tc.tile_pool(name="results", bufs=14))
        scratch = ctx.enter_context(tc.tile_pool(name="scratch", bufs=2))
        small = ctx.enter_context(tc.tile_pool(name="small", bufs=10))
        turned = ctx.enter_context(tc.psum_pool(name="turned", bufs=4))
        sums = ctx.enter_context(tc.psum_pool(name="sums", bufs=4))

        mix_rows = const.tile([P, P * PAIR], BF16)
        nc.vector.memset(mix_rows[:], 0.0)
        x_first = [inputs.tile([P, B, PAIR * P], BF16, name="x_first%d" % u) for u in range(HALVES)]
        x_rest = [inputs.tile([P, B, K_PASS], BF16, name="x_rest%d" % g) for g in range(1, PASSES)]

        def load_x(tile, seqs, first_k):
            nc.sync.dma_start(
                out=tile,
                in_=x[seqs, :, first_k : first_k + tile.shape[2]].rearrange("b s k -> s b k"),
            )

        for half in (slice(0, B // 2), slice(B // 2, B)):
            load_x(x_first[0][:, half, :], half, 0)
            if half.start == 0:
                nc.sync.dma_start(
                    out=mix_rows[0 : PASSES * HALVES, :], in_=x_k.rearrange("(a w) -> a w", w=P * PAIR)
                )
        load_x(x_first[1][:], slice(0, B), PAIR * P)
        for g in range(1, PASSES):
            load_x(x_rest[g - 1][:], slice(0, B), g * K_PASS)

        def x_words(a, b):
            g, u = divmod(a, HALVES)
            if g == 0:
                return x_first[u][:, b, :].bitcast(F32)
            return x_rest[g - 1][:, b, u * PAIR * P : (u + 1) * PAIR * P].bitcast(F32)

        w_sb = [inputs.tile([P, C], BF16, name="w_sb%d" % r) for r in range(C // P)]
        gain = const.tile([P, C], BF16)
        for r in range(C // P):
            nc.sync.dma_start(out=w_sb[r][:], in_=Wk[r * P : (r + 1) * P, :])
            if r == HEAD_CHUNKS * ROW_TILES - 1:
                nc.sync.dma_start(out=gain[:], in_=k_k.partition_broadcast(P))

        ident = const.tile([P, P], F32)
        make_identity(nc, ident[:])
        warm = const.tile([P, 1], F32)
        nc.vector.memset(warm[:], 1.0)
        nc.scalar.activation(out=warm[:], in_=warm[:], func=ACT.Abs_reciprocal_sqrt)
        prev_term = [
            const.tile([P, PAIR, B, T + 1], F32, name="prev_term%d" % i) for i in range(PASSES)
        ]
        for i in range(PASSES):
            nc.vector.memset(prev_term[i][:, :, :, 0:1], 0.0)
        mix = const.tile([P, PASSES * PACK], F32)
        keep = const.tile([P, PASSES * PACK], F32)
        mix_turned = turned.tile([P, P], F32, name="mix_turned", tag="bank")
        nc.tensor.transpose(mix_turned[:], mix_rows[:].bitcast(F32), ident[:])
        nc.vector.tensor_copy(out=mix[:], in_=mix_turned[:].bitcast(BF16)[:, 0 : PASSES * PACK])
        nc.vector.tensor_scalar(
            out=keep[:], in0=mix[:], scalar1=-1.0, scalar2=1.0, op0=ALU.mult, op1=ALU.add
        )

        x_codes = const.tile([P, PASSES, B * T], U32, align_bytes=64)
        x_scales = const.tile([P, PASSES, B * T], U8, align_bytes=64)

        x_turned = {}

        def turn_x(a):
            g, u = divmod(a, HALVES)
            ends = a in (0, PASSES * HALVES - 1)
            parts = [range(0, B // 2), range(B // 2, B)] if ends else [range(B)]
            x_turned[a] = []
            for seqs in parts:
                pool = turned if u == 0 else sums
                bank = pool.tile([P, len(seqs), T], F32, name="x_turned", tag="bank")
                for i, b in enumerate(seqs):
                    nc.tensor.transpose(bank[:, i, :], x_words(a, b), ident[:])
                x_turned[a].append((seqs, bank))

        def mix_x(g):
            planes = x_work.tile([P, PACK, B * T], BF16)
            for u in range(HALVES):
                a = HALVES * g + u
                shifted = prev_term[a % PASSES]
                for seqs, bank in x_turned[a]:
                    x_halves = bank[:].bitcast(BF16).rearrange("p b (s e) -> p b s e", e=PAIR)
                    now = slice(seqs.start, seqs.stop)
                    for e in range(PAIR):
                        col = PAIR * a + e
                        nc.scalar.activation(
                            out=shifted[:, e, now, 1 : T + 1],
                            in_=x_halves[:, :, :, e],
                            func=ACT.Copy,
                            scale=mix[:, col : col + 1],
                        )
                    for e in range(PAIR):
                        col = PAIR * a + e
                        nc.vector.scalar_tensor_tensor(
                            out=planes[:, PAIR * u + e, now.start * T : now.stop * T].rearrange(
                                "p (b s) -> p b s", b=len(seqs)
                            ),
                            in0=x_halves[:, :, :, e],
                            scalar=keep[:, col : col + 1],
                            in1=shifted[:, e, now, 0:T],
                            op0=ALU.mult,
                            op1=ALU.add,
                        )
            return planes

        def regroup_x(g, planes):
            x_grouped = x_work.tile([P, B * T, PACK], BF16, align_bytes=64)
            if g < GPSIMD_PASSES:
                nc.gpsimd.tensor_scalar(
                    out=x_grouped[:],
                    in0=planes[:].rearrange("p t c -> p c t"),
                    scalar1=1.0,
                    scalar2=0.0,
                    op0=ALU.mult,
                    op1=ALU.add,
                )
            else:
                nc.vector.tensor_copy(
                    out=x_grouped[:].rearrange("p (c i) t -> p c t i", i=4),
                    in_=planes[:].rearrange("p t (c i) -> p c t i", i=4),
                )
            return x_grouped

        def quantise_x(g, x_grouped):
            nc.vector.quantize_mx(
                out=x_codes[:, g, :].bitcast(FP8X4),
                scales=x_scales[:, g, :],
                in_=x_grouped[:].rearrange("p c t -> p (c t)"),
            )

        def new_w_chunk():
            return {
                "grouped": w_work.tile([P, PASSES, N_CHUNK, PACK], BF16, name="w_grouped", align_bytes=64),
                "codes": w_work.tile([P, PASSES, N_CHUNK], U32, name="w_codes", align_bytes=64),
                "scales": w_work.tile([P, PASSES, N_CHUNK], U8, name="w_scales", align_bytes=64),
            }

        def turn_w(n, g, chunk, last_copy):
            w_words = chunk["grouped"][:].bitcast(F32)
            for first in range(0, ROW_TILES, BANK_TILES):
                bank = turned.tile([P, HALVES, BANK_TILES, P], F32, name="w_turned", tag="bank")
                for j in range(BANK_TILES):
                    rows = w_sb[ROW_TILES * n + first + j][:].bitcast(F32)
                    for u in range(HALVES):
                        a = HALVES * g + u
                        nc.tensor.transpose(bank[:, u, j, :], rows[:, a * P : (a + 1) * P], ident[:])
                copy = last_copy if first + BANK_TILES == ROW_TILES else nc.scalar.copy
                copy(
                    out=w_words[:, g, first * P : (first + BANK_TILES) * P, :],
                    in_=bank[:].rearrange("p u j o -> p (j o) u"),
                )

        def quantise_w(g, chunk):
            nc.vector.quantize_mx(
                out=chunk["codes"][:, g, :].bitcast(FP8X4),
                scales=chunk["scales"][:, g, :],
                in_=chunk["grouped"][:, g, :, :].rearrange("p c t -> p (c t)"),
            )

        def multiply_pass(b, g, chunk, acc):
            toks = slice(b * T, (b + 1) * T)
            nc.tensor.matmul_mx(
                out=acc[:],
                lhsT=x_codes[:, g, toks].bitcast(FP8X4),
                lhsT_scale=x_scales[:, g, toks],
                rhs=chunk["codes"][:, g, :].bitcast(FP8X4),
                rhs_scale=chunk["scales"][:, g, :],
                start=(g == 0),
                stop=(g == PASSES - 1),
            )

        def multiply(b, chunk):
            acc = sums.tile([P, N_CHUNK], F32, name="acc", tag="bank")
            for g in range(PASSES):
                multiply_pass(b, g, chunk, acc)
            return acc

        def times_gain(n, acc):
            kk = results.tile([P, HEADS, HEAD], F32)
            nc.vector.tensor_tensor(
                out=kk[:].rearrange("p h d -> p (h d)"),
                in0=acc[:],
                in1=gain[:, n * N_CHUNK : (n + 1) * N_CHUNK],
                op=ALU.mult,
            )
            return kk

        def square_heads(tiles):
            squares = scratch.tile([P, STEP, HEADS, HEAD], F32)
            sumsq = small.tile([P, STEP, HEADS], F32)
            for i, (b, kk) in enumerate(tiles):
                for h in range(HEADS):
                    nc.scalar.activation(
                        out=squares[:, i, h, :], in_=kk[:, h, :], func=ACT.Square,
                        accum_out=sumsq[:, i, h : h + 1],
                    )
            return sumsq

        def invert(tiles, sumsq):
            used = slice(0, len(tiles))
            inverse = small.tile([P, STEP, HEADS], F32)
            nc.scalar.activation(
                out=inverse[:, used, :], in_=sumsq[:, used, :], func=ACT.Abs_reciprocal_sqrt
            )
            return inverse

        def store(n, b, kk):
            nc.sync.dma_start(
                out=out[b, :, n * N_CHUNK : (n + 1) * N_CHUNK],
                in_=kk[:].rearrange("p h d -> p (h d)"),
            )

        def cap(inverse):
            capped = small.tile([P, STEP, HEADS], F32)
            nc.vector.tensor_scalar_min(out=capped[:], in0=inverse[:], scalar1=1e12)
            return capped

        def scale_on_gpsimd(n, b, kk, capped, i):
            nc.gpsimd.tensor_tensor(
                out=kk[:],
                in0=kk[:],
                in1=capped[:, i, :].unsqueeze(2).to_broadcast([P, HEADS, HEAD]),
                op=ALU.mult,
            )
            store(n, b, kk)

        def scale_on_scalar(n, b, kk, capped, i):
            for h in range(HEADS):
                nc.scalar.activation(
                    out=kk[:, h, :], in_=kk[:, h, :], func=ACT.Copy, scale=capped[:, i, h : h + 1]
                )
            store(n, b, kk)

        def scale_on_vector(n, b, kk, inverse, i):
            nc.vector.scalar_tensor_tensor(
                out=kk[:],
                in0=inverse[:, i, :].unsqueeze(2).to_broadcast([P, HEADS, HEAD]),
                scalar=1e12,
                in1=kk[:],
                op0=ALU.min,
                op1=ALU.mult,
            )
            store(n, b, kk)

        chunks = [new_w_chunk() for n in range(HEAD_CHUNKS)]
        mixed = []
        regrouped = []
        for a in range((PASSES - 1) * HALVES):
            turn_x(a)
        for g in range(PASSES):
            mixed.append(mix_x(g))
            if g < GPSIMD_PASSES:
                regrouped.append(regroup_x(g, mixed[g]))
            if g == 0:
                for a in range((PASSES - 1) * HALVES, PASSES * HALVES):
                    turn_x(a)
        first_accs = []

        def first_pass(g):
            if g >= GPSIMD_PASSES and len(regrouped) == g:
                regrouped.append(regroup_x(g, mixed[g]))
            if g < GPSIMD_PASSES:
                quantise_x(g, regrouped[g])
                quantise_w(g, chunks[0])
            else:
                quantise_w(g, chunks[0])
                quantise_x(g, regrouped[g])
            if g == 0:
                for b in range(B):
                    acc = sums.tile([P, N_CHUNK], F32, name="acc", tag="bank")
                    first_accs.append(acc)
            for b in range(B):
                multiply_pass(b, g, chunks[0], first_accs[b])

        turn_w(0, 0, chunks[0], nc.scalar.copy)
        turn_w(0, 1, chunks[0], nc.scalar.copy)
        turn_w(0, 2, chunks[0], nc.scalar.copy)
        turn_w(0, 3, chunks[0], nc.scalar.copy)
        first_pass(0)
        turn_w(1, 0, chunks[1], nc.scalar.copy)
        first_pass(1)
        turn_w(1, 1, chunks[1], nc.scalar.copy)
        first_pass(2)
        turn_w(1, 2, chunks[1], nc.scalar.copy)
        turn_w(1, 3, chunks[1], nc.scalar.copy)
        first_pass(3)

        waiting = None
        squared = None
        late = None
        for n in range(CHUNKS - 1):
            turn_next = HEAD_CHUNKS <= n + 1 < CHUNKS
            if turn_next:
                chunks.append(new_w_chunk())
            for first in range(0, B, STEP):
                step = range(first, first + STEP)
                if turn_next:
                    for g in step:
                        turn_w(n + 1, g, chunks[n + 1], nc.scalar.copy if False else nc.vector.tensor_copy)
                accs = [first_accs[b] if n == 0 else multiply(b, chunks[n]) for b in step]
                if squared is not None:
                    inverse = invert(squared[1], squared[2])
                if late is not None:
                    scale_on_scalar(*late)
                    late = None
                tiles = None
                if waiting is not None:
                    m, seqs, sums_of = waiting
                    tiles = [(b, times_gain(m, acc)) for b, acc in zip(seqs, sums_of)]
                    sumsq = square_heads(tiles)
                for g in step:
                    quantise_w(g, chunks[n + 1])
                if squared is not None:
                    capped = cap(inverse)
                    (b0, kk0), (b1, kk1) = squared[1]
                    scale_on_gpsimd(squared[0], b0, kk0, capped, 0)
                    late = (squared[0], b1, kk1, capped, 1)
                squared = None if tiles is None else (m, tiles, sumsq)
                waiting = (n, step, accs)
        n = CHUNKS - 1
        m, seqs, sums_of = waiting
        accs = [multiply(b, chunks[n]) for b in range(STEP)]
        inverse = invert(squared[1], squared[2])
        if late is not None:
            scale_on_scalar(*late)
        last = [(b, times_gain(m, acc)) for b, acc in zip(seqs, sums_of)]
        accs += [multiply(b, chunks[n]) for b in range(STEP, B)]
        (b0, kk0), (b1, kk1) = squared[1]
        sumsq = square_heads(last)
        kks = [times_gain(n, accs[0])]
        scale_on_vector(squared[0], b0, kk0, inverse, 0)
        kks.append(times_gain(n, accs[1]))
        scale_on_vector(squared[0], b1, kk1, inverse, 1)
        inverse = invert(last, sumsq)
        sums0 = square_heads([(0, kks[0])])
        kks.append(times_gain(n, accs[2]))
        scale_on_vector(m, last[0][0], last[0][1], inverse, 0)
        sums1 = square_heads([(1, kks[1])])
        inv0 = invert([0], sums0)
        kks.append(times_gain(n, accs[3]))
        scale_on_vector(m, last[1][0], last[1][1], inverse, 1)
        sums2 = square_heads([(2, kks[2])])
        inv1 = invert([0], sums1)
        scale_on_vector(n, 0, kks[0], inv0, 0)
        scale_on_vector(n, 1, kks[1], inv1, 0)
        sums3 = square_heads([(3, kks[3])])
        inv2 = invert([0], sums2)
        scale_on_vector(n, 2, kks[2], inv2, 0)
        inv3 = invert([0], sums3)
        scale_on_vector(n, 3, kks[3], inv3, 0)
